import numpy as np
import ml_dtypes


def mxq(x, axis, fmt="e4m3"):
    dtype, down = {"e4m3": (ml_dtypes.float8_e4m3fn, 7), "e5m2": (ml_dtypes.float8_e5m2, 14)}[fmt]
    v = np.moveaxis(np.asarray(x, np.float32).astype(ml_dtypes.bfloat16).astype(np.float64), axis, -1)
    blocks = v.reshape(v.shape[:-1] + (-1, 32))
    amax = np.abs(blocks).max(-1, keepdims=True)
    byte = np.maximum(np.where(amax > 0, np.frexp(amax)[1] - 1 + 127, 0) - down, 1)
    scale = np.exp2(byte - 127.0)
    codes = (blocks / scale).astype(np.float32).astype(dtype).astype(np.float64)
    return np.moveaxis((codes * scale).reshape(v.shape), -1, axis)


WIDE = False


def mx_kscale(k):
    if not WIDE:
        return np.ones(k)
    levels = np.array([10, -10, 5, -5, 0])
    a = np.random.permutation(np.resize(levels, k // 512 * 4)).reshape(k // 512, 4)
    idx = np.arange(k)
    return np.exp2(a[idx // 512, idx % 128 // 32])


BF16 = ml_dtypes.bfloat16


def bf(x):
    return np.asarray(x, np.float32).astype(BF16)


def f64(x):
    return np.asarray(x).astype(np.float64)


E2M1 = np.array([0.0, 0.5, 1.0, 1.5, 2.0, 3.0, 4.0, 6.0, -0.0, -0.5, -1.0, -1.5, -2.0, -3.0, -4.0, -6.0])


def pack_weight(w, fmt):
    k, n = w.shape
    w = f64(bf(w)).reshape(k // 32, 32, n)
    amax = np.abs(w).max(1)
    if fmt == "e4m3":
        byte = np.frexp(amax)[1] - 1 + 127 - 7
    else:
        mant, ex = np.frexp(amax / 6.0)
        byte = np.where(mant > 0.5, ex, ex - 1) + 127
    byte = np.clip(np.where(amax > 0, byte, 1), 1, 254)
    scaled = (w * np.exp2(127.0 - byte)[:, None, :]).reshape(k, n).astype(np.float32)
    by_word = np.ascontiguousarray(scaled.reshape(k // 512, 128, 4, n).transpose(0, 1, 3, 2))
    if fmt == "e4m3":
        words = by_word.astype(ml_dtypes.float8_e4m3fn).view(np.uint8)
    else:
        c = by_word.astype(ml_dtypes.float4_e2m1fn).view(np.uint8) & 0xF
        words = c[..., 0::2] | (c[..., 1::2] << 4)
    return np.ascontiguousarray(words), np.ascontiguousarray(byte.astype(np.uint8).reshape(k // 512, 16, n))


def unpack_weight(words, scales, fmt):
    g, p, n, _ = words.shape
    if fmt == "e4m3":
        vals = np.ascontiguousarray(words).view(ml_dtypes.float8_e4m3fn).astype(np.float64)
    else:
        nib = np.empty((g, p, n, 4), np.uint8)
        nib[..., 0::2] = words & 0xF
        nib[..., 1::2] = words >> 4
        vals = E2M1[nib]
    vals = vals * np.repeat(np.exp2(scales.astype(np.float64) - 127.0), 8, axis=1)[..., None]
    return vals.transpose(0, 1, 3, 2).reshape(g * 512, n)

def pack4(w):
    words, scales = pack_weight(w, "e2m1")
    return words.reshape(words.shape[0], 128, -1), scales


def unpack4(words, scales):
    return unpack_weight(words.reshape(words.shape[0], 128, -1, 2), scales, "e2m1")


B, IN_DIM, LAT, OUT_DIM = 8192, 256, 256, 512
G = IN_DIM + LAT


def sigmoid(v):
    return 1.0 / (1.0 + np.exp(-v))


def setup_inputs():
    s = mx_kscale(G)
    x_t = bf(np.random.standard_normal((B, IN_DIM)) * s[:IN_DIM])
    h_t = bf(np.random.standard_normal((B, LAT)) * 0.85 * s[IN_DIM:])
    Wy_words, Wy_scales = pack4(np.random.standard_normal((G, OUT_DIM)) * 0.8 / np.sqrt(G) / s[:, None])
    by = bf(np.random.standard_normal(OUT_DIM) * 0.2)
    Wo_words, Wo_scales = pack4(np.random.standard_normal((G, OUT_DIM)) * 0.8 / np.sqrt(G) / s[:, None])
    bo = bf(np.random.standard_normal(OUT_DIM) * 0.2)
    return {
        "x_t": x_t,
        "h_t": h_t,
        "Wy_words": Wy_words,
        "Wy_scales": Wy_scales,
        "by": by,
        "Wo_words": Wo_words,
        "Wo_scales": Wo_scales,
        "bo": bo,
    }


def reference(x_t, h_t, Wy_words, Wy_scales, by, Wo_words, Wo_scales, bo):
    xq = mxq(np.concatenate([f64(x_t), f64(h_t)], axis=1), 1, "e4m3")
    y_hat = np.tanh((xq @ unpack4(Wy_words, Wy_scales)) + f64(by))
    o_t = sigmoid((xq @ unpack4(Wo_words, Wo_scales)) + f64(bo))
    return y_hat * o_t

@@ -1,0 +1,210 @@
+from contextlib import ExitStack
+
+import concourse.mybir as mybir
+from concourse.masks import make_identity
+
+F32 = mybir.dt.float32
+BF16 = mybir.dt.bfloat16
+I32 = mybir.dt.int32
+U32 = mybir.dt.uint32
+U8 = mybir.dt.uint8
+FP8X4 = mybir.dt.float8_e4m3fn_x4
+FP4X4 = mybir.dt.float4_e2m1fn_x4
+ACT = mybir.ActivationFunctionType
+MULT = mybir.AluOpType.mult
+
+P = 128
+PACK = 4
+BATCH = 8192
+IN_DIM = 256
+K = 512
+OUT_DIM = 512
+BLOCK = 512
+ROW_TILES = BLOCK // P
+BLOCKS = BATCH // BLOCK
+ROUND_TILES = 2
+ROUNDS_PER_BLOCK = OUT_DIM // (P * ROUND_TILES)
+ROUNDS = BLOCKS * ROUNDS_PER_BLOCK
+HALF = BLOCK // ROUNDS_PER_BLOCK
+GATES = 2
+GATE_FUNC = (ACT.Sigmoid, ACT.Tanh)
+
+X_LEAD = 4
+OUT_LAG = 3
+GPSIMD_COLS = 3 * P
+
+FLOPS = 2 * GATES * BATCH * K * OUT_DIM
+
+
+def tile_gatel0rdcell_pb_t_kernel(
+    tc, x_t, h_t, Wy_words, Wy_scales, by, Wo_words, Wo_scales, bo, out
+):
+    nc = tc.nc
+    with ExitStack() as ctx:
+        ctx.enter_context(tc.manual_schedule())
+        consts = ctx.enter_context(tc.tile_pool(name="consts", bufs=1))
+        xh_pool = ctx.enter_context(tc.tile_pool(name="xh", bufs=BLOCKS))
+        grouped_pool = ctx.enter_context(tc.tile_pool(name="grouped", bufs=2))
+        mx_pool = ctx.enter_context(tc.tile_pool(name="mx", bufs=3))
+        gate_pool = ctx.enter_context(tc.tile_pool(name="gates", bufs=4))
+        prod_pool = ctx.enter_context(tc.tile_pool(name="prod", bufs=4))
+        out_pool = ctx.enter_context(tc.tile_pool(name="out", bufs=3))
+        psum_x = ctx.enter_context(tc.psum_pool(name="psum_x", bufs=2))
+        psum_z = ctx.enter_context(tc.psum_pool(name="psum_z", bufs=4))
+        psum_o = ctx.enter_context(tc.psum_pool(name="psum_o", bufs=2))
+
+        xh = []
+
+        def load_block(blk):
+            rows = slice(blk * BLOCK, (blk + 1) * BLOCK)
+            xh_blk = xh_pool.tile([P, ROW_TILES, K], BF16, name="xh_blk")
+            nc.sync.dma_start(
+                out=xh_blk[:, :, 0:IN_DIM], in_=x_t[rows, :].rearrange("(p s) k -> p s k", s=ROW_TILES)
+            )
+            nc.sync.dma_start(
+                out=xh_blk[:, :, IN_DIM:K], in_=h_t[rows, :].rearrange("(p s) k -> p s k", s=ROW_TILES)
+            )
+            xh.append(xh_blk)
+
+        load_block(0)
+
+        w_words = consts.tile([P, GATES, 2 * OUT_DIM], U8, name="w_words", align_bytes=64)
+        w_planes = consts.tile([P, GATES, OUT_DIM], U8, name="w_planes", align_bytes=64)
+        nc.vector.memset(w_planes[:].rearrange("p g n -> p (g n)").bitcast(I32), 0)
+        for g, (words, scales) in enumerate(((Wo_words, Wo_scales), (Wy_words, Wy_scales))):
+            nc.sync.dma_start(out=w_words[:, g, :].bitcast(I32), in_=words[0].bitcast(I32))
+            for quad in range(4):
+                nc.sync.dma_start(
+                    out=w_planes[32 * quad : 32 * quad + 4, g, :].bitcast(I32),
+                    in_=scales[0, 4 * quad : 4 * quad + 4, :].bitcast(I32),
+                )
+
+        bias_rows = consts.tile([P, P], BF16, name="bias_rows")
+        nc.vector.memset(bias_rows[:], 0.0)
+        for g, bias in enumerate((bo, by)):
+            nc.sync.dma_start(
+                out=bias_rows[4 * g : 4 * g + 4, :], in_=bias.rearrange("(r c) -> r c", c=P)
+            )
+
+        for blk in range(1, BLOCKS):
+            load_block(blk)
+
+        ident = consts.tile([P, P], F32, name="ident")
+        make_identity(nc, ident[:])
+
+        grouped = {}
+        x_words = {}
+        x_planes = {}
+        gates = {}
+        prods = {}
+        out_rows = {}
+
+        def transpose_x(x_round):
+            blk, half = divmod(x_round, ROUNDS_PER_BLOCK)
+            if half == 0:
+                grouped[blk] = grouped_pool.tile([P, BLOCK * PACK], BF16, name="grouped", align_bytes=64)
+            xT = psum_x.tile([P, 2, HALF], F32, name="xT")
+            for i in range(HALF // P):
+                pairs_of_k = xh[blk][:, half * (HALF // P) + i, :].bitcast(F32)
+                for u in range(2):
+                    nc.tensor.transpose(xT[:, u, i * P : (i + 1) * P], pairs_of_k[:, u : K // 2 : 2], ident[:])
+            words_of_j = grouped[blk][:].bitcast(F32).rearrange("p (j u) -> p j u", u=2)
+            nc.vector.tensor_copy(
+                out=words_of_j[:, half * HALF : (half + 1) * HALF, :], in_=xT[:].rearrange("p u j -> p j u")
+            )
+
+        def quantise_x(x_round):
+            blk, half = divmod(x_round, ROUNDS_PER_BLOCK)
+            if half == 0:
+                x_words[blk] = mx_pool.tile([P, BLOCK], U32, name="x_words", align_bytes=64)
+                x_planes[blk] = mx_pool.tile([P, BLOCK], U8, name="x_planes", align_bytes=64)
+            cols = slice(half * HALF, (half + 1) * HALF)
+            nc.vector.quantize_mx(
+                out=x_words[blk][:, cols].bitcast(FP8X4),
+                scales=x_planes[blk][:, cols],
+                in_=grouped[blk][:, half * HALF * PACK : (half + 1) * HALF * PACK],
+            )
+
+        def bias_columns():
+            bias_rows_f32 = consts.tile([P, P], F32, name="bias_rows_f32")
+            nc.vector.tensor_copy(out=bias_rows_f32[:], in_=bias_rows[:])
+            bias_ps = psum_o.tile([P, ROW_TILES, P], F32, name="bias_ps", tag="oT")
+            nc.tensor.transpose(bias_ps[:, 0, :], bias_rows_f32[:], ident[:])
+            cols = consts.tile([P, 4 * GATES], F32, name="bias_cols")
+            nc.vector.tensor_copy(out=cols[:], in_=bias_ps[:, 0, 0 : 4 * GATES])
+            return cols
+
+        def compute_gates(rnd):
+            blk, half = divmod(rnd, ROUNDS_PER_BLOCK)
+            gates[rnd] = gate_pool.tile([P, GATES, ROUND_TILES, BLOCK], F32, name="gates")
+            for i in range(ROUND_TILES):
+                n_tile = half * ROUND_TILES + i
+                for g in range(GATES):
+                    z = psum_z.tile([P, BLOCK], F32, name="z")
+                    nc.tensor.matmul_mx(
+                        out=z[:],
+                        lhsT=w_words[:, g, 2 * P * n_tile : 2 * P * (n_tile + 1)].bitcast(FP4X4),
+                        lhsT_scale=w_planes[:, g, P * n_tile : P * (n_tile + 1)],
+                        rhs=x_words[blk][:].bitcast(FP8X4),
+                        rhs_scale=x_planes[blk][:],
+                        start=True,
+                        stop=True,
+                    )
+                    nc.scalar.activation(
+                        out=gates[rnd][:, g, i, :],
+                        in_=z[:],
+                        func=GATE_FUNC[g],
+                        bias=bias_cols[:, 4 * g + n_tile : 4 * g + n_tile + 1],
+                        scale=1.0,
+                    )
+
+        def multiply_gates(rnd):
+            prods[rnd] = prod_pool.tile([P, ROUND_TILES, BLOCK], F32, name="prod")
+            o_gate = gates[rnd][:, 0, :, :]
+            y_gate = gates[rnd][:, 1, :, :]
+            nc.gpsimd.tensor_tensor(
+                out=prods[rnd][:, :, 0:GPSIMD_COLS],
+                in0=y_gate[:, :, 0:GPSIMD_COLS],
+                in1=o_gate[:, :, 0:GPSIMD_COLS],
+                op=MULT,
+            )
+            nc.vector.tensor_tensor(
+                out=prods[rnd][:, :, GPSIMD_COLS:BLOCK],
+                in0=y_gate[:, :, GPSIMD_COLS:BLOCK],
+                in1=o_gate[:, :, GPSIMD_COLS:BLOCK],
+                op=MULT,
+            )
+
+        def transpose_out(rnd):
+            blk, half = divmod(rnd, ROUNDS_PER_BLOCK)
+            if half == 0:
+                out_rows[blk] = out_pool.tile([P, ROW_TILES, OUT_DIM], F32, name="out_rows")
+            for i in range(ROUND_TILES):
+                n_tile = half * ROUND_TILES + i
+                oT = psum_o.tile([P, ROW_TILES, P], F32, name="oT")
+                for s in range(ROW_TILES):
+                    nc.tensor.transpose(oT[:, s, :], prods[rnd][:, i, s * P : (s + 1) * P], ident[:])
+                nc.vector.tensor_copy(out=out_rows[blk][:, :, n_tile * P : (n_tile + 1) * P], in_=oT[:])
+            if half == ROUNDS_PER_BLOCK - 1:
+                nc.sync.dma_start(
+                    out=out[blk * BLOCK : (blk + 1) * BLOCK, :].rearrange("(p s) n -> p s n", s=ROW_TILES),
+                    in_=out_rows[blk][:],
+                )
+
+        for x_round in range(X_LEAD):
+            transpose_x(x_round)
+            if x_round >= 1:
+                quantise_x(x_round - 1)
+        bias_cols = bias_columns()
+
+        for step in range(ROUNDS + OUT_LAG):
+            if 0 <= step - 1 < ROUNDS:
+                multiply_gates(step - 1)
+            if step + X_LEAD - 1 < ROUNDS:
+                quantise_x(step + X_LEAD - 1)
+            if step < ROUNDS:
+                compute_gates(step)
+            if 0 <= step - OUT_LAG < ROUNDS:
+                transpose_out(step - OUT_LAG)
+            if step + X_LEAD < ROUNDS:
+                transpose_x(step + X_LEAD)

@@ -29,7 +29,7 @@ HALF = BLOCK // ROUNDS_PER_BLOCK
 GATES = 2
 GATE_FUNC = (ACT.Sigmoid, ACT.Tanh)
 
-X_LEAD = 4
+X_LEAD = 3
 OUT_LAG = 3
 GPSIMD_COLS = 3 * P
 
@@ -48,10 +48,9 @@ def tile_gatel0rdcell_pb_t_kernel(
         mx_pool = ctx.enter_context(tc.tile_pool(name="mx", bufs=3))
         gate_pool = ctx.enter_context(tc.tile_pool(name="gates", bufs=4))
         prod_pool = ctx.enter_context(tc.tile_pool(name="prod", bufs=4))
-        out_pool = ctx.enter_context(tc.tile_pool(name="out", bufs=3))
-        psum_x = ctx.enter_context(tc.psum_pool(name="psum_x", bufs=2))
-        psum_z = ctx.enter_context(tc.psum_pool(name="psum_z", bufs=4))
-        psum_o = ctx.enter_context(tc.psum_pool(name="psum_o", bufs=2))
+        out_pool = ctx.enter_context(tc.tile_pool(name="out", bufs=4))
+        psum_z = ctx.enter_context(tc.psum_pool(name="psum_z", bufs=5))
+        psum_t = ctx.enter_context(tc.psum_pool(name="psum_t", bufs=3))
 
         xh = []
 
@@ -66,6 +65,13 @@ def tile_gatel0rdcell_pb_t_kernel(
             )
             xh.append(xh_blk)
 
+        bias_rows = consts.tile([P, P], BF16, name="bias_rows")
+        nc.vector.memset(bias_rows[:], 0.0)
+        for g, bias in enumerate((bo, by)):
+            nc.sync.dma_start(
+                out=bias_rows[4 * g : 4 * g + 4, :], in_=bias.rearrange("(r c) -> r c", c=P)
+            )
+
         load_block(0)
 
         w_words = consts.tile([P, GATES, 2 * OUT_DIM], U8, name="w_words", align_bytes=64)
@@ -79,31 +85,28 @@ def tile_gatel0rdcell_pb_t_kernel(
                     in_=scales[0, 4 * quad : 4 * quad + 4, :].bitcast(I32),
                 )
 
-        bias_rows = consts.tile([P, P], BF16, name="bias_rows")
-        nc.vector.memset(bias_rows[:], 0.0)
-        for g, bias in enumerate((bo, by)):
-            nc.sync.dma_start(
-                out=bias_rows[4 * g : 4 * g + 4, :], in_=bias.rearrange("(r c) -> r c", c=P)
-            )
-
         for blk in range(1, BLOCKS):
             load_block(blk)
 
         ident = consts.tile([P, P], F32, name="ident")
         make_identity(nc, ident[:])
 
+        table_in = consts.tile([P, 1], F32, name="table_in")
+        table_out = consts.tile([P, 1], F32, name="table_out")
+        nc.vector.memset(table_in[:], 0.0)
+        nc.scalar.activation(out=table_out[:], in_=table_in[:], func=ACT.Sigmoid)
+
         grouped = {}
         x_words = {}
         x_planes = {}
         gates = {}
         prods = {}
-        out_rows = {}
 
         def transpose_x(x_round):
             blk, half = divmod(x_round, ROUNDS_PER_BLOCK)
             if half == 0:
                 grouped[blk] = grouped_pool.tile([P, BLOCK * PACK], BF16, name="grouped", align_bytes=64)
-            xT = psum_x.tile([P, 2, HALF], F32, name="xT")
+            xT = psum_t.tile([P, 2, HALF], F32, name="xT", tag="turned")
             for i in range(HALF // P):
                 pairs_of_k = xh[blk][:, half * (HALF // P) + i, :].bitcast(F32)
                 for u in range(2):
@@ -128,7 +131,7 @@ def tile_gatel0rdcell_pb_t_kernel(
         def bias_columns():
             bias_rows_f32 = consts.tile([P, P], F32, name="bias_rows_f32")
             nc.vector.tensor_copy(out=bias_rows_f32[:], in_=bias_rows[:])
-            bias_ps = psum_o.tile([P, ROW_TILES, P], F32, name="bias_ps", tag="oT")
+            bias_ps = psum_t.tile([P, ROW_TILES, P], F32, name="bias_ps", tag="turned")
             nc.tensor.transpose(bias_ps[:, 0, :], bias_rows_f32[:], ident[:])
             cols = consts.tile([P, 4 * GATES], F32, name="bias_cols")
             nc.vector.tensor_copy(out=cols[:], in_=bias_ps[:, 0, 0 : 4 * GATES])
@@ -177,28 +180,30 @@ def tile_gatel0rdcell_pb_t_kernel(
 
         def transpose_out(rnd):
             blk, half = divmod(rnd, ROUNDS_PER_BLOCK)
-            if half == 0:
-                out_rows[blk] = out_pool.tile([P, ROW_TILES, OUT_DIM], F32, name="out_rows")
+            out_rows = out_pool.tile([P, ROW_TILES, ROUND_TILES * P], F32, name="out_rows")
             for i in range(ROUND_TILES):
-                n_tile = half * ROUND_TILES + i
-                oT = psum_o.tile([P, ROW_TILES, P], F32, name="oT")
+                oT = psum_t.tile([P, ROW_TILES, P], F32, name="oT", tag="turned")
                 for s in range(ROW_TILES):
                     nc.tensor.transpose(oT[:, s, :], prods[rnd][:, i, s * P : (s + 1) * P], ident[:])
-                nc.vector.tensor_copy(out=out_rows[blk][:, :, n_tile * P : (n_tile + 1) * P], in_=oT[:])
-            if half == ROUNDS_PER_BLOCK - 1:
-                nc.sync.dma_start(
-                    out=out[blk * BLOCK : (blk + 1) * BLOCK, :].rearrange("(p s) n -> p s n", s=ROW_TILES),
-                    in_=out_rows[blk][:],
-                )
+                nc.vector.tensor_copy(out=out_rows[:, :, i * P : (i + 1) * P], in_=oT[:])
+            features = slice(half * ROUND_TILES * P, (half + 1) * ROUND_TILES * P)
+            nc.sync.dma_start(
+                out=out[blk * BLOCK : (blk + 1) * BLOCK, features].rearrange("(p s) n -> p s n", s=ROW_TILES),
+                in_=out_rows[:],
+            )
 
-        for x_round in range(X_LEAD):
-            transpose_x(x_round)
-            if x_round >= 1:
-                quantise_x(x_round - 1)
         bias_cols = bias_columns()
+        for x_round in range(ROUNDS_PER_BLOCK):
+            transpose_x(x_round)
+        for x_round in range(ROUNDS_PER_BLOCK):
+            quantise_x(x_round)
+        compute_gates(0)
+        for x_round in range(ROUNDS_PER_BLOCK, X_LEAD + 1):
+            transpose_x(x_round)
+        quantise_x(X_LEAD - 1)
 
-        for step in range(ROUNDS + OUT_LAG):
-            if 0 <= step - 1 < ROUNDS:
+        for step in range(1, ROUNDS + OUT_LAG):
+            if step - 1 < ROUNDS:
                 multiply_gates(step - 1)
             if step + X_LEAD - 1 < ROUNDS:
                 quantise_x(step + X_LEAD - 1)

@@ -29,7 +29,7 @@ HALF = BLOCK // ROUNDS_PER_BLOCK
 GATES = 2
 GATE_FUNC = (ACT.Sigmoid, ACT.Tanh)
 
-X_LEAD = 3
+X_LEAD = 4
 OUT_LAG = 3
 GPSIMD_COLS = 3 * P
 
@@ -200,7 +200,8 @@ def tile_gatel0rdcell_pb_t_kernel(
         compute_gates(0)
         for x_round in range(ROUNDS_PER_BLOCK, X_LEAD + 1):
             transpose_x(x_round)
-        quantise_x(X_LEAD - 1)
+        for x_round in range(ROUNDS_PER_BLOCK, X_LEAD):
+            quantise_x(x_round)
 
         for step in range(1, ROUNDS + OUT_LAG):
             if step - 1 < ROUNDS:

@@ -31,6 +31,7 @@ GATE_FUNC = (ACT.Sigmoid, ACT.Tanh)
 
 X_LEAD = 4
 OUT_LAG = 3
+LOAD_LEAD = 4
 GPSIMD_COLS = 3 * P
 
 FLOPS = 2 * GATES * BATCH * K * OUT_DIM
@@ -48,7 +49,7 @@ def tile_gatel0rdcell_pb_t_kernel(
         mx_pool = ctx.enter_context(tc.tile_pool(name="mx", bufs=3))
         gate_pool = ctx.enter_context(tc.tile_pool(name="gates", bufs=4))
         prod_pool = ctx.enter_context(tc.tile_pool(name="prod", bufs=4))
-        out_pool = ctx.enter_context(tc.tile_pool(name="out", bufs=4))
+        out_pool = ctx.enter_context(tc.tile_pool(name="out", bufs=6))
         psum_z = ctx.enter_context(tc.psum_pool(name="psum_z", bufs=5))
         psum_t = ctx.enter_context(tc.psum_pool(name="psum_t", bufs=3))
 
@@ -85,7 +86,7 @@ def tile_gatel0rdcell_pb_t_kernel(
                     in_=scales[0, 4 * quad : 4 * quad + 4, :].bitcast(I32),
                 )
 
-        for blk in range(1, BLOCKS):
+        for blk in range(1, LOAD_LEAD + 1):
             load_block(blk)
 
         ident = consts.tile([P, P], F32, name="ident")
@@ -204,6 +205,9 @@ def tile_gatel0rdcell_pb_t_kernel(
             quantise_x(x_round)
 
         for step in range(1, ROUNDS + OUT_LAG):
+            blk, half = divmod(step, ROUNDS_PER_BLOCK)
+            if half == 0 and blk + LOAD_LEAD < BLOCKS:
+                load_block(blk + LOAD_LEAD)
             if step - 1 < ROUNDS:
                 multiply_gates(step - 1)
             if step + X_LEAD - 1 < ROUNDS:

@@ -32,7 +32,7 @@ GATE_FUNC = (ACT.Sigmoid, ACT.Tanh)
 X_LEAD = 4
 OUT_LAG = 3
 LOAD_LEAD = 4
-GPSIMD_COLS = 3 * P
+GPSIMD_COLS = 2 * P
 
 FLOPS = 2 * GATES * BATCH * K * OUT_DIM
 
@@ -166,16 +166,17 @@ def tile_gatel0rdcell_pb_t_kernel(
             prods[rnd] = prod_pool.tile([P, ROUND_TILES, BLOCK], F32, name="prod")
             o_gate = gates[rnd][:, 0, :, :]
             y_gate = gates[rnd][:, 1, :, :]
+            nc.gpsimd.tensor_tensor(out=prods[rnd][:, 0, :], in0=y_gate[:, 0, :], in1=o_gate[:, 0, :], op=MULT)
             nc.gpsimd.tensor_tensor(
-                out=prods[rnd][:, :, 0:GPSIMD_COLS],
-                in0=y_gate[:, :, 0:GPSIMD_COLS],
-                in1=o_gate[:, :, 0:GPSIMD_COLS],
+                out=prods[rnd][:, 1, 0:GPSIMD_COLS],
+                in0=y_gate[:, 1, 0:GPSIMD_COLS],
+                in1=o_gate[:, 1, 0:GPSIMD_COLS],
                 op=MULT,
             )
             nc.vector.tensor_tensor(
-                out=prods[rnd][:, :, GPSIMD_COLS:BLOCK],
-                in0=y_gate[:, :, GPSIMD_COLS:BLOCK],
-                in1=o_gate[:, :, GPSIMD_COLS:BLOCK],
+                out=prods[rnd][:, 1, GPSIMD_COLS:BLOCK],
+                in0=y_gate[:, 1, GPSIMD_COLS:BLOCK],
+                in1=o_gate[:, 1, GPSIMD_COLS:BLOCK],
                 op=MULT,
             )
 

@@ -32,7 +32,6 @@ GATE_FUNC = (ACT.Sigmoid, ACT.Tanh)
 X_LEAD = 4
 OUT_LAG = 3
 LOAD_LEAD = 4
-GPSIMD_COLS = 2 * P
 
 FLOPS = 2 * GATES * BATCH * K * OUT_DIM
 
@@ -167,18 +166,7 @@ def tile_gatel0rdcell_pb_t_kernel(
             o_gate = gates[rnd][:, 0, :, :]
             y_gate = gates[rnd][:, 1, :, :]
             nc.gpsimd.tensor_tensor(out=prods[rnd][:, 0, :], in0=y_gate[:, 0, :], in1=o_gate[:, 0, :], op=MULT)
-            nc.gpsimd.tensor_tensor(
-                out=prods[rnd][:, 1, 0:GPSIMD_COLS],
-                in0=y_gate[:, 1, 0:GPSIMD_COLS],
-                in1=o_gate[:, 1, 0:GPSIMD_COLS],
-                op=MULT,
-            )
-            nc.vector.tensor_tensor(
-                out=prods[rnd][:, 1, GPSIMD_COLS:BLOCK],
-                in0=y_gate[:, 1, GPSIMD_COLS:BLOCK],
-                in1=o_gate[:, 1, GPSIMD_COLS:BLOCK],
-                op=MULT,
-            )
+            nc.vector.tensor_tensor(out=prods[rnd][:, 1, :], in0=y_gate[:, 1, :], in1=o_gate[:, 1, :], op=MULT)
 
         def transpose_out(rnd):
             blk, half = divmod(rnd, ROUNDS_PER_BLOCK)

@@ -32,6 +32,7 @@ GATE_FUNC = (ACT.Sigmoid, ACT.Tanh)
 X_LEAD = 4
 OUT_LAG = 3
 LOAD_LEAD = 4
+SCALAR_EVERY = 4
 
 FLOPS = 2 * GATES * BATCH * K * OUT_DIM
 
@@ -112,9 +113,8 @@ def tile_gatel0rdcell_pb_t_kernel(
                 for u in range(2):
                     nc.tensor.transpose(xT[:, u, i * P : (i + 1) * P], pairs_of_k[:, u : K // 2 : 2], ident[:])
             words_of_j = grouped[blk][:].bitcast(F32).rearrange("p (j u) -> p j u", u=2)
-            nc.vector.tensor_copy(
-                out=words_of_j[:, half * HALF : (half + 1) * HALF, :], in_=xT[:].rearrange("p u j -> p j u")
-            )
+            copy_out = nc.scalar.copy if x_round % SCALAR_EVERY == 1 else nc.vector.tensor_copy
+            copy_out(out=words_of_j[:, half * HALF : (half + 1) * HALF, :], in_=xT[:].rearrange("p u j -> p j u"))
 
         def quantise_x(x_round):
             blk, half = divmod(x_round, ROUNDS_PER_BLOCK)

@@ -31,6 +31,7 @@ GATE_FUNC = (ACT.Sigmoid, ACT.Tanh)
 
 X_LEAD = 4
 OUT_LAG = 3
+X_DONE = ROUNDS - X_LEAD
 LOAD_LEAD = 4
 SCALAR_EVERY = 4
 
@@ -168,19 +169,29 @@ def tile_gatel0rdcell_pb_t_kernel(
             nc.gpsimd.tensor_tensor(out=prods[rnd][:, 0, :], in0=y_gate[:, 0, :], in1=o_gate[:, 0, :], op=MULT)
             nc.vector.tensor_tensor(out=prods[rnd][:, 1, :], in0=y_gate[:, 1, :], in1=o_gate[:, 1, :], op=MULT)
 
-        def transpose_out(rnd):
+        def store(rnd, first_tile, tiles, out_rows):
             blk, half = divmod(rnd, ROUNDS_PER_BLOCK)
+            first = (half * ROUND_TILES + first_tile) * P
+            nc.sync.dma_start(
+                out=out[blk * BLOCK : (blk + 1) * BLOCK, first : first + tiles * P].rearrange(
+                    "(p s) n -> p s n", s=ROW_TILES
+                ),
+                in_=out_rows[:, :, first_tile * P : (first_tile + tiles) * P],
+            )
+
+        def transpose_out(rnd):
+            is_last = rnd == ROUNDS - 1
             out_rows = out_pool.tile([P, ROW_TILES, ROUND_TILES * P], F32, name="out_rows")
             for i in range(ROUND_TILES):
                 oT = psum_t.tile([P, ROW_TILES, P], F32, name="oT", tag="turned")
                 for s in range(ROW_TILES):
                     nc.tensor.transpose(oT[:, s, :], prods[rnd][:, i, s * P : (s + 1) * P], ident[:])
-                nc.vector.tensor_copy(out=out_rows[:, :, i * P : (i + 1) * P], in_=oT[:])
-            features = slice(half * ROUND_TILES * P, (half + 1) * ROUND_TILES * P)
-            nc.sync.dma_start(
-                out=out[blk * BLOCK : (blk + 1) * BLOCK, features].rearrange("(p s) n -> p s n", s=ROW_TILES),
-                in_=out_rows[:],
-            )
+                copy_out = nc.scalar.copy if is_last and i == 0 else nc.vector.tensor_copy
+                copy_out(out=out_rows[:, :, i * P : (i + 1) * P], in_=oT[:])
+                if is_last:
+                    store(rnd, i, 1, out_rows)
+            if not is_last:
+                store(rnd, 0, ROUND_TILES, out_rows)
 
         bias_cols = bias_columns()
         for x_round in range(ROUNDS_PER_BLOCK):
@@ -193,7 +204,10 @@ def tile_gatel0rdcell_pb_t_kernel(
         for x_round in range(ROUNDS_PER_BLOCK, X_LEAD):
             quantise_x(x_round)
 
-        for step in range(1, ROUNDS + OUT_LAG):
+        def turned_after(step):
+            return step + 1 - max(1, OUT_LAG - max(0, step - X_DONE))
+
+        for step in range(1, ROUNDS + 1):
             blk, half = divmod(step, ROUNDS_PER_BLOCK)
             if half == 0 and blk + LOAD_LEAD < BLOCKS:
                 load_block(blk + LOAD_LEAD)
@@ -203,7 +217,7 @@ def tile_gatel0rdcell_pb_t_kernel(
                 quantise_x(step + X_LEAD - 1)
             if step < ROUNDS:
                 compute_gates(step)
-            if 0 <= step - OUT_LAG < ROUNDS:
-                transpose_out(step - OUT_LAG)
+            for rnd in range(max(0, turned_after(step - 1)), turned_after(step)):
+                transpose_out(rnd)
             if step + X_LEAD < ROUNDS:
                 transpose_x(step + X_LEAD)

@@ -33,7 +33,7 @@ X_LEAD = 4
 OUT_LAG = 3
 X_DONE = ROUNDS - X_LEAD
 LOAD_LEAD = 4
-SCALAR_EVERY = 4
+SCALAR_EVERY = 3
 
 FLOPS = 2 * GATES * BATCH * K * OUT_DIM
 

from contextlib import ExitStack

import concourse.mybir as mybir
from concourse.masks import make_identity

F32 = mybir.dt.float32
BF16 = mybir.dt.bfloat16
I32 = mybir.dt.int32
U32 = mybir.dt.uint32
U8 = mybir.dt.uint8
FP8X4 = mybir.dt.float8_e4m3fn_x4
FP4X4 = mybir.dt.float4_e2m1fn_x4
ACT = mybir.ActivationFunctionType
MULT = mybir.AluOpType.mult

P = 128
PACK = 4
BATCH = 8192
IN_DIM = 256
K = 512
OUT_DIM = 512
BLOCK = 512
ROW_TILES = BLOCK // P
BLOCKS = BATCH // BLOCK
ROUND_TILES = 2
ROUNDS_PER_BLOCK = OUT_DIM // (P * ROUND_TILES)
ROUNDS = BLOCKS * ROUNDS_PER_BLOCK
HALF = BLOCK // ROUNDS_PER_BLOCK
GATES = 2
GATE_FUNC = (ACT.Sigmoid, ACT.Tanh)

X_LEAD = 4
OUT_LAG = 3
X_DONE = ROUNDS - X_LEAD
LOAD_LEAD = 4
SCALAR_EVERY = 3

FLOPS = 2 * GATES * BATCH * K * OUT_DIM


def tile_gatel0rdcell_pb_t_kernel(
    tc, x_t, h_t, Wy_words, Wy_scales, by, Wo_words, Wo_scales, bo, out
):
    nc = tc.nc
    with ExitStack() as ctx:
        ctx.enter_context(tc.manual_schedule())
        consts = ctx.enter_context(tc.tile_pool(name="consts", bufs=1))
        xh_pool = ctx.enter_context(tc.tile_pool(name="xh", bufs=BLOCKS))
        grouped_pool = ctx.enter_context(tc.tile_pool(name="grouped", bufs=2))
        mx_pool = ctx.enter_context(tc.tile_pool(name="mx", bufs=3))
        gate_pool = ctx.enter_context(tc.tile_pool(name="gates", bufs=4))
        prod_pool = ctx.enter_context(tc.tile_pool(name="prod", bufs=4))
        out_pool = ctx.enter_context(tc.tile_pool(name="out", bufs=6))
        psum_z = ctx.enter_context(tc.psum_pool(name="psum_z", bufs=5))
        psum_t = ctx.enter_context(tc.psum_pool(name="psum_t", bufs=3))

        xh = []

        def load_block(blk):
            rows = slice(blk * BLOCK, (blk + 1) * BLOCK)
            xh_blk = xh_pool.tile([P, ROW_TILES, K], BF16, name="xh_blk")
            nc.sync.dma_start(
                out=xh_blk[:, :, 0:IN_DIM], in_=x_t[rows, :].rearrange("(p s) k -> p s k", s=ROW_TILES)
            )
            nc.sync.dma_start(
                out=xh_blk[:, :, IN_DIM:K], in_=h_t[rows, :].rearrange("(p s) k -> p s k", s=ROW_TILES)
            )
            xh.append(xh_blk)

        bias_rows = consts.tile([P, P], BF16, name="bias_rows")
        nc.vector.memset(bias_rows[:], 0.0)
        for g, bias in enumerate((bo, by)):
            nc.sync.dma_start(
                out=bias_rows[4 * g : 4 * g + 4, :], in_=bias.rearrange("(r c) -> r c", c=P)
            )

        load_block(0)

        w_words = consts.tile([P, GATES, 2 * OUT_DIM], U8, name="w_words", align_bytes=64)
        w_planes = consts.tile([P, GATES, OUT_DIM], U8, name="w_planes", align_bytes=64)
        nc.vector.memset(w_planes[:].rearrange("p g n -> p (g n)").bitcast(I32), 0)
        for g, (words, scales) in enumerate(((Wo_words, Wo_scales), (Wy_words, Wy_scales))):
            nc.sync.dma_start(out=w_words[:, g, :].bitcast(I32), in_=words[0].bitcast(I32))
            for quad in range(4):
                nc.sync.dma_start(
                    out=w_planes[32 * quad : 32 * quad + 4, g, :].bitcast(I32),
                    in_=scales[0, 4 * quad : 4 * quad + 4, :].bitcast(I32),
                )

        for blk in range(1, LOAD_LEAD + 1):
            load_block(blk)

        ident = consts.tile([P, P], F32, name="ident")
        make_identity(nc, ident[:])

        table_in = consts.tile([P, 1], F32, name="table_in")
        table_out = consts.tile([P, 1], F32, name="table_out")
        nc.vector.memset(table_in[:], 0.0)
        nc.scalar.activation(out=table_out[:], in_=table_in[:], func=ACT.Sigmoid)

        grouped = {}
        x_words = {}
        x_planes = {}
        gates = {}
        prods = {}

        def transpose_x(x_round):
            blk, half = divmod(x_round, ROUNDS_PER_BLOCK)
            if half == 0:
                grouped[blk] = grouped_pool.tile([P, BLOCK * PACK], BF16, name="grouped", align_bytes=64)
            xT = psum_t.tile([P, 2, HALF], F32, name="xT", tag="turned")
            for i in range(HALF // P):
                pairs_of_k = xh[blk][:, half * (HALF // P) + i, :].bitcast(F32)
                for u in range(2):
                    nc.tensor.transpose(xT[:, u, i * P : (i + 1) * P], pairs_of_k[:, u : K // 2 : 2], ident[:])
            words_of_j = grouped[blk][:].bitcast(F32).rearrange("p (j u) -> p j u", u=2)
            copy_out = nc.scalar.copy if x_round % SCALAR_EVERY == 1 else nc.vector.tensor_copy
            copy_out(out=words_of_j[:, half * HALF : (half + 1) * HALF, :], in_=xT[:].rearrange("p u j -> p j u"))

        def quantise_x(x_round):
            blk, half = divmod(x_round, ROUNDS_PER_BLOCK)
            if half == 0:
                x_words[blk] = mx_pool.tile([P, BLOCK], U32, name="x_words", align_bytes=64)
                x_planes[blk] = mx_pool.tile([P, BLOCK], U8, name="x_planes", align_bytes=64)
            cols = slice(half * HALF, (half + 1) * HALF)
            nc.vector.quantize_mx(
                out=x_words[blk][:, cols].bitcast(FP8X4),
                scales=x_planes[blk][:, cols],
                in_=grouped[blk][:, half * HALF * PACK : (half + 1) * HALF * PACK],
            )

        def bias_columns():
            bias_rows_f32 = consts.tile([P, P], F32, name="bias_rows_f32")
            nc.vector.tensor_copy(out=bias_rows_f32[:], in_=bias_rows[:])
            bias_ps = psum_t.tile([P, ROW_TILES, P], F32, name="bias_ps", tag="turned")
            nc.tensor.transpose(bias_ps[:, 0, :], bias_rows_f32[:], ident[:])
            cols = consts.tile([P, 4 * GATES], F32, name="bias_cols")
            nc.vector.tensor_copy(out=cols[:], in_=bias_ps[:, 0, 0 : 4 * GATES])
            return cols

        def compute_gates(rnd):
            blk, half = divmod(rnd, ROUNDS_PER_BLOCK)
            gates[rnd] = gate_pool.tile([P, GATES, ROUND_TILES, BLOCK], F32, name="gates")
            for i in range(ROUND_TILES):
                n_tile = half * ROUND_TILES + i
                for g in range(GATES):
                    z = psum_z.tile([P, BLOCK], F32, name="z")
                    nc.tensor.matmul_mx(
                        out=z[:],
                        lhsT=w_words[:, g, 2 * P * n_tile : 2 * P * (n_tile + 1)].bitcast(FP4X4),
                        lhsT_scale=w_planes[:, g, P * n_tile : P * (n_tile + 1)],
                        rhs=x_words[blk][:].bitcast(FP8X4),
                        rhs_scale=x_planes[blk][:],
                        start=True,
                        stop=True,
                    )
                    nc.scalar.activation(
                        out=gates[rnd][:, g, i, :],
                        in_=z[:],
                        func=GATE_FUNC[g],
                        bias=bias_cols[:, 4 * g + n_tile : 4 * g + n_tile + 1],
                        scale=1.0,
                    )

        def multiply_gates(rnd):
            prods[rnd] = prod_pool.tile([P, ROUND_TILES, BLOCK], F32, name="prod")
            o_gate = gates[rnd][:, 0, :, :]
            y_gate = gates[rnd][:, 1, :, :]
            nc.gpsimd.tensor_tensor(out=prods[rnd][:, 0, :], in0=y_gate[:, 0, :], in1=o_gate[:, 0, :], op=MULT)
            nc.vector.tensor_tensor(out=prods[rnd][:, 1, :], in0=y_gate[:, 1, :], in1=o_gate[:, 1, :], op=MULT)

        def store(rnd, first_tile, tiles, out_rows):
            blk, half = divmod(rnd, ROUNDS_PER_BLOCK)
            first = (half * ROUND_TILES + first_tile) * P
            nc.sync.dma_start(
                out=out[blk * BLOCK : (blk + 1) * BLOCK, first : first + tiles * P].rearrange(
                    "(p s) n -> p s n", s=ROW_TILES
                ),
                in_=out_rows[:, :, first_tile * P : (first_tile + tiles) * P],
            )

        def transpose_out(rnd):
            is_last = rnd == ROUNDS - 1
            out_rows = out_pool.tile([P, ROW_TILES, ROUND_TILES * P], F32, name="out_rows")
            for i in range(ROUND_TILES):
                oT = psum_t.tile([P, ROW_TILES, P], F32, name="oT", tag="turned")
                for s in range(ROW_TILES):
                    nc.tensor.transpose(oT[:, s, :], prods[rnd][:, i, s * P : (s + 1) * P], ident[:])
                copy_out = nc.scalar.copy if is_last and i == 0 else nc.vector.tensor_copy
                copy_out(out=out_rows[:, :, i * P : (i + 1) * P], in_=oT[:])
                if is_last:
                    store(rnd, i, 1, out_rows)
            if not is_last:
                store(rnd, 0, ROUND_TILES, out_rows)

        bias_cols = bias_columns()
        for x_round in range(ROUNDS_PER_BLOCK):
            transpose_x(x_round)
        for x_round in range(ROUNDS_PER_BLOCK):
            quantise_x(x_round)
        compute_gates(0)
        for x_round in range(ROUNDS_PER_BLOCK, X_LEAD + 1):
            transpose_x(x_round)
        for x_round in range(ROUNDS_PER_BLOCK, X_LEAD):
            quantise_x(x_round)

        def turned_after(step):
            return step + 1 - max(1, OUT_LAG - max(0, step - X_DONE))

        for step in range(1, ROUNDS + 1):
            blk, half = divmod(step, ROUNDS_PER_BLOCK)
            if half == 0 and blk + LOAD_LEAD < BLOCKS:
                load_block(blk + LOAD_LEAD)
            if step - 1 < ROUNDS:
                multiply_gates(step - 1)
            if step + X_LEAD - 1 < ROUNDS:
                quantise_x(step + X_LEAD - 1)
            if step < ROUNDS:
                compute_gates(step)
            for rnd in range(max(0, turned_after(step - 1)), turned_after(step)):
                transpose_out(rnd)
            if step + X_LEAD < ROUNDS:
                transpose_x(step + X_LEAD)
